import numpy as np
import ml_dtypes


def mxq(x, axis, fmt="e4m3"):
    dtype, down = {"e4m3": (ml_dtypes.float8_e4m3fn, 7), "e5m2": (ml_dtypes.float8_e5m2, 14)}[fmt]
    v = np.moveaxis(np.asarray(x, np.float32).astype(ml_dtypes.bfloat16).astype(np.float64), axis, -1)
    blocks = v.reshape(v.shape[:-1] + (-1, 32))
    amax = np.abs(blocks).max(-1, keepdims=True)
    byte = np.maximum(np.where(amax > 0, np.frexp(amax)[1] - 1 + 127, 0) - down, 1)
    scale = np.exp2(byte - 127.0)
    codes = (blocks / scale).astype(np.float32).astype(dtype).astype(np.float64)
    return np.moveaxis((codes * scale).reshape(v.shape), -1, axis)


WIDE = False


def mx_kscale(k):
    if not WIDE:
        return np.ones(k)
    levels = np.array([10, -10, 5, -5, 0])
    if k % 512:
        return np.exp2(np.random.permutation(np.resize(levels, k // 32))).repeat(32)
    a = np.empty((k // 512, 16))
    for p in range(k // 512):
        a[p, :8] = np.random.permutation(np.resize(levels, 8))
        for g in range(8):
            far = levels[np.abs(levels - a[p, g]) >= 10]
            a[p, g + 8] = far[np.random.randint(len(far))]
    return np.exp2(a.ravel()).repeat(32)


BF16 = ml_dtypes.bfloat16


def bf(x):
    return np.asarray(x, np.float32).astype(BF16)


def f64(x):
    return np.asarray(x).astype(np.float64)


E2M1 = np.array([0.0, 0.5, 1.0, 1.5, 2.0, 3.0, 4.0, 6.0, -0.0, -0.5, -1.0, -1.5, -2.0, -3.0, -4.0, -6.0])


def pack_weight(w, fmt):
    k, n = w.shape
    w = f64(bf(w)).reshape(k // 32, 32, n)
    amax = np.abs(w).max(1)
    if fmt == "e4m3":
        byte = np.frexp(amax)[1] - 1 + 127 - 7
    else:
        mant, ex = np.frexp(amax / 6.0)
        byte = np.where(mant > 0.5, ex, ex - 1) + 127
    byte = np.clip(np.where(amax > 0, byte, 1), 1, 254)
    scaled = (w * np.exp2(127.0 - byte)[:, None, :]).reshape(k, n).astype(np.float32)
    by_word = np.ascontiguousarray(scaled.reshape(k // 512, 128, 4, n).transpose(0, 1, 3, 2))
    if fmt == "e4m3":
        words = by_word.astype(ml_dtypes.float8_e4m3fn).view(np.uint8)
    else:
        c = by_word.astype(ml_dtypes.float4_e2m1fn).view(np.uint8) & 0xF
        words = c[..., 0::2] | (c[..., 1::2] << 4)
    return np.ascontiguousarray(words), np.ascontiguousarray(byte.astype(np.uint8).reshape(k // 512, 16, n))


def unpack_weight(words, scales, fmt):
    g, p, n, _ = words.shape
    if fmt == "e4m3":
        vals = np.ascontiguousarray(words).view(ml_dtypes.float8_e4m3fn).astype(np.float64)
    else:
        nib = np.empty((g, p, n, 4), np.uint8)
        nib[..., 0::2] = words & 0xF
        nib[..., 1::2] = words >> 4
        vals = E2M1[nib]
    vals = vals * np.repeat(np.exp2(scales.astype(np.float64) - 127.0), 8, axis=1)[..., None]
    return vals.transpose(0, 1, 3, 2).reshape(g * 512, n)
def pack4(w):
    words, scales = pack_weight(w, "e2m1")
    return words.reshape(words.shape[0], 128, -1), scales


def unpack4(words, scales):
    return unpack_weight(words.reshape(words.shape[0], 128, -1, 2), scales, "e2m1")


B, T, D, H, HD, F = 4, 1024, 512, 8, 64, 128
A = H * HD
EPS = 1e-5
ERF_H = 0.5
ERF_N = 14


def layernorm(x, g, b):
    mu = np.mean(x, axis=-1, keepdims=True)
    var = np.mean(np.square(x - mu), axis=-1, keepdims=True)
    return (x - mu) / np.sqrt(var + EPS) * g + b


def erf(z):
    acc = np.zeros_like(z)
    for n in range(ERF_N):
        tn = (n + 0.5) * ERF_H
        acc = acc + np.exp(-tn * tn) / (tn * tn + z * z)
    return np.tanh(np.pi * z / ERF_H) - 2.0 * ERF_H * z * np.exp(-z * z) / np.pi * acc


def gelu_erf(v):
    return 0.5 * v * (1.0 + erf(v / np.sqrt(2.0)))


def draw0():
    s, t = mx_kscale(A), mx_kscale(D)
    attn = bf(np.random.standard_normal((B, T, A)) * 0.25 * s)
    x = bf(np.random.standard_normal((B, T, D)) + 0.5 * np.random.standard_normal((B, T, 1)))
    w_out_words, w_out_scales = pack4(np.random.standard_normal((A, D)) * 2.0 / np.sqrt(A) / s[:, None])
    b_out = bf(0.1 * np.random.standard_normal(D))
    ln2_g = bf((1.0 + 0.1 * np.random.standard_normal(D)) * t)
    ln2_b = bf(0.1 * np.random.standard_normal(D) * t)
    w1_words, w1_scales = pack4(np.random.standard_normal((D, F)) / np.sqrt(D) / t[:, None])
    b1 = bf(0.2 * np.random.standard_normal(F))
    return {"attn": attn,
            "x": x,
            "w_out_words": w_out_words,
            "w_out_scales": w_out_scales,
            "b_out": b_out,
            "ln2_g": ln2_g,
            "ln2_b": ln2_b,
            "w1_words": w1_words,
            "w1_scales": w1_scales,
            "b1": b1}


def core(attn, x, w_out_words, w_out_scales, b_out, ln2_g, ln2_b, w1_words, w1_scales, b1):
    x_mid = f64(x) + ((mxq(f64(attn), 2, "e4m3") @ unpack4(w_out_words, w_out_scales)) + f64(b_out))
    h2 = layernorm(x_mid, f64(ln2_g), f64(ln2_b))
    hid = gelu_erf((mxq(h2, 2, "e4m3") @ unpack4(w1_words, w1_scales)) + f64(b1))
    return x_mid, hid


def e4m3fn_bytes(y):
    return np.clip(np.asarray(y, np.float64), -448.0, 448.0).astype(np.float32).astype(ml_dtypes.float8_e4m3fn).view(np.uint8)


def e4m3fn_values(b):
    return np.asarray(b, np.uint8).view(ml_dtypes.float8_e4m3fn).astype(np.float64)


def setup_inputs():
    d = draw0()
    x0 = np.asarray(d['attn']).astype(np.float64)
    s = (np.max(np.abs(x0), axis=(0, 1), keepdims=True) / 448.0).astype(np.float32)
    out = {}
    for k, v in d.items():
        if k == 'attn':
            out['attn_bytes'] = e4m3fn_bytes(x0 / s.astype(np.float64))
            out['attn_scale'] = s
        else:
            out[k] = v
    return out


def reference(attn_bytes, attn_scale, x, w_out_words, w_out_scales, b_out, ln2_g, ln2_b, w1_words, w1_scales, b1):
    return core(e4m3fn_values(attn_bytes) * attn_scale.astype(np.float64), x, w_out_words, w_out_scales, b_out, ln2_g, ln2_b, w1_words, w1_scales, b1)

@@ -1,0 +1,347 @@
+from contextlib import ExitStack
+
+import concourse.mybir as mybir
+from concourse.masks import make_identity
+
+P = 128
+PACK = 4
+D = 512
+F = 128
+TOKENS = 4096
+TILES = TOKENS // P
+NT = 2
+GROUPS = TILES // NT
+W = NT * P
+EPS = 1e-5
+
+FLOPS = 2 * TOKENS * D * D + 2 * TOKENS * D * F
+
+F32 = mybir.dt.float32
+BF16 = mybir.dt.bfloat16
+U32 = mybir.dt.uint32
+I32 = mybir.dt.int32
+U8 = mybir.dt.uint8
+FP8 = mybir.dt.float8_e4m3fn
+FP8X4 = mybir.dt.float8_e4m3fn_x4
+FP4X4 = mybir.dt.float4_e2m1fn_x4
+ADD = mybir.AluOpType.add
+SUB = mybir.AluOpType.subtract
+MULT = mybir.AluOpType.mult
+POW = mybir.AluOpType.pow
+ACT = mybir.ActivationFunctionType
+
+CHUNKS = [2, 2, 4, 8, 8, 8]
+
+
+def tile_transformerblock_pb_t_w4_kernel(
+    tc, attn_bytes, attn_scale, x, w_out_words, w_out_scales, b_out, ln2_g, ln2_b, w1_words, w1_scales, b1, out_0, out_1
+):
+    nc = tc.nc
+    bytes_v = attn_bytes.rearrange("b t k -> (b t) k").rearrange("(p j) k -> p j k", p=P)
+    x_v = x.rearrange("b t d -> (b t) d").rearrange("(p j) d -> p j d", p=P)
+    mid_v = out_0.rearrange("b t d -> (b t) d").rearrange("(p j) d -> p j d", p=P)
+    hid_v = out_1.rearrange("b t f -> (b t) f").rearrange("(p j) f -> p j f", p=P)
+
+    with ExitStack() as ctx:
+        keep = ctx.enter_context(tc.tile_pool(name="keep", bufs=1))
+        work = ctx.enter_context(tc.tile_pool(name="work", bufs=3))
+        psum = ctx.enter_context(tc.psum_pool(name="psum", bufs=1))
+
+        scale_t = keep.tile([P, NT, D], F32, name="scale_t", align_bytes=64)
+        nc.scalar.dma_start(out=scale_t[:, 0, :], in_=attn_scale.rearrange("o t k -> (o t k)").partition_broadcast(P))
+
+        wscale = keep.tile([P, D + F], U8, name="wscale", align_bytes=64)
+        nc.vector.memset(wscale[:].bitcast(I32), 0)
+        b_rows = keep.tile([P, P], F32, name="b_rows")
+        nc.vector.memset(b_rows[:], 0.0)
+        ident = keep.tile([P, P], F32, name="ident")
+        make_identity(nc, ident[:])
+        expo = keep.tile([P, NT], F32, name="expo")
+        nc.gpsimd.memset(expo[:], -0.5)
+        warm = keep.tile([P, 1], F32, name="warm")
+        nc.vector.memset(warm[:], 0.0)
+        warm_o = keep.tile([P, 1], F32, name="warm_o")
+        nc.scalar.activation(out=warm_o[:], in_=warm[:], func=ACT.Gelu)
+
+        b_raw = keep.tile([P, P], BF16, name="b_raw")
+        nc.scalar.dma_start(out=b_raw[0:4, :], in_=b_out.rearrange("(j m) -> j m", m=P))
+        g_raw = keep.tile([P, PACK], BF16, name="g_raw")
+        nc.scalar.dma_start(out=g_raw[:], in_=ln2_g.rearrange("(p t) -> p t", t=PACK))
+        lb_raw = keep.tile([P, PACK], BF16, name="lb_raw")
+        nc.scalar.dma_start(out=lb_raw[:], in_=ln2_b.rearrange("(p t) -> p t", t=PACK))
+        b1_t = keep.tile([P, NT, F], BF16, name="b1_t")
+        nc.scalar.dma_start(out=b1_t[:, 0, :], in_=b1.partition_broadcast(P))
+
+        byte_tiles = []
+        x_tiles = []
+        w_words = keep.tile([P, 2 * D], U8, name="w_words", align_bytes=64)
+        w1_t = keep.tile([P, 2 * F], U8, name="w1_t", align_bytes=64)
+        start = 0
+        for ci, n in enumerate(CHUNKS):
+            byte_t = keep.tile([P, n * D], U8, name="bytes%d" % ci, align_bytes=64)
+            nc.sync.dma_start(out=byte_t[:].rearrange("p (j k) -> p j k", k=D), in_=bytes_v[:, start : start + n, :])
+            if ci == 0:
+                nc.sync.dma_start(out=w_words[:], in_=w_out_words[0])
+                for q in range(4):
+                    nc.sync.dma_start(
+                        out=wscale[32 * q : 32 * q + 4, 0:D].bitcast(I32),
+                        in_=w_out_scales[0, 4 * q : 4 * q + 4, :].bitcast(I32),
+                    )
+            x_t = keep.tile([P, n, D], BF16, name="x%d" % ci)
+            nc.sync.dma_start(out=x_t[:], in_=x_v[:, start : start + n, :])
+            if ci == 1:
+                nc.sync.dma_start(out=w1_t[:], in_=w1_words[0])
+                for q in range(4):
+                    nc.sync.dma_start(
+                        out=wscale[32 * q : 32 * q + 4, D : D + F].bitcast(I32),
+                        in_=w1_scales[0, 4 * q : 4 * q + 4, :].bitcast(I32),
+                    )
+            for j in range(n):
+                byte_tiles.append((byte_t, j))
+                x_tiles.append((x_t, j))
+            start += n
+
+        nc.gpsimd.tensor_copy(out=b_rows[0:4, :], in_=b_raw[0:4, :])
+        g_f = keep.tile([P, PACK], F32, name="g_f")
+        nc.gpsimd.tensor_copy(out=g_f[:], in_=g_raw[:])
+        lb_f = keep.tile([P, PACK], F32, name="lb_f")
+        nc.gpsimd.tensor_copy(out=lb_f[:], in_=lb_raw[:])
+        for j in range(1, NT):
+            nc.gpsimd.tensor_copy(out=b1_t[:, j, :], in_=b1_t[:, 0, :])
+        bp = psum.tile([P, P], F32, tag="hid", name="bp")
+        nc.tensor.transpose(bp[:], b_rows[:], ident[:])
+        b_col = keep.tile([P, PACK], F32, name="b_col")
+        nc.scalar.copy(out=b_col[:], in_=bp[:, 0:PACK])
+        for j in range(1, NT):
+            nc.scalar.copy(out=scale_t[:, j, :], in_=scale_t[:, 0, :])
+
+        att = {}
+        atp = {}
+        codes = {}
+        ptp = {}
+        pts = {}
+        xmp = {}
+        xms = {}
+        stat = {}
+        xhs = {}
+        xhp = {}
+        pls = {}
+        hqs = {}
+        codes2 = {}
+        hps = {}
+        hvs = {}
+
+        def widen(g):
+            t = work.tile([P, NT * D], BF16, name="att", align_bytes=64)
+            att[g] = t
+            bt, j0 = byte_tiles[NT * g]
+            if g == 0:
+                for j in range(NT):
+                    nc.vector.tensor_tensor(
+                        out=t[:, j * D : (j + 1) * D],
+                        in0=bt[:, (j0 + j) * D : (j0 + j + 1) * D].bitcast(FP8),
+                        in1=scale_t[:, 0, :],
+                        op=MULT,
+                    )
+            else:
+                nc.vector.tensor_tensor(
+                    out=t[:],
+                    in0=bt[:, j0 * D : (j0 + NT) * D].bitcast(FP8),
+                    in1=scale_t[:].rearrange("p j k -> p (j k)"),
+                    op=MULT,
+                )
+
+        def turn_attn(g):
+            t = psum.tile([P, NT, 2, P], F32, tag="at", name="at")
+            atp[g] = t
+            words = att[g][:].bitcast(F32)
+            for j in range(NT):
+                for u in range(2):
+                    nc.tensor.transpose(t[:, j, u, :], words[:, 256 * j + u : 256 * (j + 1) : 2], ident[:])
+
+        def copy_attn(g):
+            t = work.tile([P, W * PACK], BF16, name="grp", align_bytes=64)
+            att[g] = t
+            nc.scalar.copy(
+                out=t[:].bitcast(F32).rearrange("p (j r u) -> p j r u", j=NT, u=2),
+                in_=atp[g][:].rearrange("p j u r -> p j r u"),
+            )
+
+        def quant_attn(g):
+            c = work.tile([P, W], U32, name="c1", align_bytes=64)
+            s = work.tile([P, W], U8, name="s1", align_bytes=64)
+            codes[g] = (c, s)
+            nc.vector.quantize_mx(out=c[:].bitcast(FP8X4), scales=s[:], in_=att[g][:])
+
+        def project(g):
+            c, s = codes[g]
+            ptp[g] = []
+            for h in range(2):
+                t = psum.tile([P, 2, W], F32, tag="pt", bufs=2, name="pt")
+                ptp[g].append(t)
+                for e in range(2):
+                    blk = 2 * h + e
+                    nc.tensor.matmul_mx(
+                        out=t[:, e, :],
+                        lhsT=w_words[:, 256 * blk : 256 * (blk + 1)].bitcast(FP4X4),
+                        lhsT_scale=wscale[:, P * blk : P * (blk + 1)],
+                        rhs=c[:].bitcast(FP8X4),
+                        rhs_scale=s[:],
+                        start=True,
+                        stop=True,
+                    )
+
+        def empty_projection(g):
+            t = work.tile([P, 4, W], F32, name="pts")
+            pts[g] = t
+            for blk in range(4):
+                nc.scalar.activation(
+                    out=t[:, blk, :], in_=ptp[g][blk // 2][:, blk % 2, :], func=ACT.Identity, bias=b_col[:, blk : blk + 1]
+                )
+
+        def turn_back(g):
+            xmp[g] = []
+            for j in range(NT):
+                t = psum.tile([P, D], F32, tag="xm", bufs=2, name="xm")
+                xmp[g].append(t)
+                for blk in range(4):
+                    nc.tensor.transpose(t[:, P * blk : P * (blk + 1)], pts[g][:, blk, P * j : P * (j + 1)], ident[:])
+
+        def residual(g):
+            t = work.tile([P, NT, D], F32, name="mid")
+            s = work.tile([P, NT], F32, name="sums")
+            xms[g] = t
+            stat[g] = s
+            for j in range(NT):
+                xt, jj = x_tiles[NT * g + j]
+                nc.vector.scalar_tensor_tensor(
+                    out=t[:, j, :],
+                    in0=xmp[g][j][:],
+                    scalar=0.0,
+                    in1=xt[:, jj, :],
+                    op0=ADD,
+                    op1=ADD,
+                    accum_out=s[:, j : j + 1],
+                )
+            nc.sync.dma_start(out=mid_v[:, NT * g : NT * (g + 1), :], in_=t[:])
+
+        def deviations(g):
+            sq = work.tile([P, NT], F32, name="sq")
+            for j in range(NT):
+                junk = work.tile([P, D], BF16, name="junk", bufs=2)
+                nc.scalar.activation(
+                    out=junk[:],
+                    in_=xms[g][:, j, :],
+                    func=ACT.Square,
+                    scale=-float(D),
+                    bias=stat[g][:, j : j + 1],
+                    accum_out=sq[:, j : j + 1],
+                )
+            mean = work.tile([P, NT], F32, name="mean")
+            nc.gpsimd.tensor_scalar(out=mean[:], in0=stat[g][:], scalar1=1.0 / D, scalar2=0.0, op0=MULT, op1=ADD)
+            var = work.tile([P, NT], F32, name="var")
+            nc.gpsimd.tensor_scalar(out=var[:], in0=sq[:], scalar1=1.0 / D**3, scalar2=EPS, op0=MULT, op1=ADD)
+            rstd = work.tile([P, NT], F32, name="rstd")
+            nc.gpsimd.tensor_tensor(out=rstd[:], in0=var[:], in1=expo[:], op=POW)
+            stat[g] = (mean, rstd)
+
+        def normalise(g):
+            t = work.tile([P, NT, D], F32, name="xh")
+            xhs[g] = t
+            mean, rstd = stat[g]
+            for j in range(NT):
+                nc.vector.tensor_scalar(
+                    out=t[:, j, :].rearrange("p (t m) -> p m t", t=PACK),
+                    in0=xms[g][:, j, :].rearrange("p (m t) -> p m t", t=PACK),
+                    scalar1=mean[:, j : j + 1],
+                    scalar2=rstd[:, j : j + 1],
+                    op0=SUB,
+                    op1=MULT,
+                )
+
+        def turn_norm(g):
+            xhp[g] = []
+            for h in range(2):
+                t = psum.tile([P, 2, W], F32, tag="xh", bufs=2, name="xhp")
+                xhp[g].append(t)
+                for e in range(2):
+                    k = 2 * h + e
+                    for j in range(NT):
+                        nc.tensor.transpose(
+                            t[:, e, P * j : P * (j + 1)], xhs[g][:, j, P * k : P * (k + 1)], ident[:]
+                        )
+
+        def gain_bias(g):
+            t = work.tile([P, PACK, W], BF16, name="planes")
+            pls[g] = t
+            for k in range(PACK):
+                nc.scalar.activation(
+                    out=t[:, k, :],
+                    in_=xhp[g][k // 2][:, k % 2, :],
+                    func=ACT.Identity,
+                    scale=g_f[:, k : k + 1],
+                    bias=lb_f[:, k : k + 1],
+                )
+
+        def interleave(g):
+            t = work.tile([P, W * PACK], BF16, name="hq", align_bytes=64)
+            hqs[g] = t
+            nc.vector.tensor_copy(
+                out=t[:].rearrange("p (c i t) -> p c t i", i=4, t=PACK),
+                in_=pls[g][:].rearrange("p t (c i) -> p c t i", i=4),
+            )
+
+        def quant_norm(g):
+            c = work.tile([P, W], U32, name="c2", align_bytes=64)
+            s = work.tile([P, W], U8, name="s2", align_bytes=64)
+            codes2[g] = (c, s)
+            nc.vector.quantize_mx(out=c[:].bitcast(FP8X4), scales=s[:], in_=hqs[g][:])
+
+        def project2(g):
+            c, s = codes2[g]
+            t = psum.tile([P, NT, F], F32, tag="hid", name="hp")
+            hps[g] = t
+            for j in range(NT):
+                nc.tensor.matmul_mx(
+                    out=t[:, j, :],
+                    lhsT=c[:, P * j : P * (j + 1)].bitcast(FP8X4),
+                    lhsT_scale=s[:, P * j : P * (j + 1)],
+                    rhs=w1_t[:].bitcast(FP4X4),
+                    rhs_scale=wscale[:, D : D + F],
+                    start=True,
+                    stop=True,
+                )
+
+        def bias2(g):
+            t = work.tile([P, NT, F], F32, name="hv")
+            hvs[g] = t
+            nc.vector.tensor_tensor(out=t[:], in0=hps[g][:], in1=b1_t[:], op=ADD)
+
+        def gelu(g):
+            t = work.tile([P, NT, F], F32, name="ho")
+            nc.scalar.activation(out=t[:], in_=hvs[g][:], func=ACT.Gelu)
+            nc.sync.dma_start(out=hid_v[:, NT * g : NT * (g + 1), :], in_=t[:])
+
+        def run(step, g):
+            if 0 <= g < GROUPS:
+                step(g)
+
+        if True:
+            for i in range(-2, GROUPS + 2):
+                run(residual, i)
+                run(gain_bias, i - 1)
+                run(project2, i - 2)
+                run(project, i + 1)
+                run(deviations, i)
+                run(widen, i + 2)
+                run(bias2, i - 2)
+                run(empty_projection, i + 1)
+                run(turn_attn, i + 2)
+                run(interleave, i - 1)
+                run(turn_back, i + 1)
+                run(copy_attn, i + 2)
+                run(normalise, i)
+                run(quant_norm, i - 1)
+                run(gelu, i - 2)
+                run(turn_norm, i)
+                run(quant_attn, i + 2)

@@ -10,8 +10,6 @@ F = 128
 TOKENS = 4096
 TILES = TOKENS // P
 NT = 2
-GROUPS = TILES // NT
-W = NT * P
 EPS = 1e-5
 
 FLOPS = 2 * TOKENS * D * D + 2 * TOKENS * D * F
@@ -30,7 +28,11 @@ MULT = mybir.AluOpType.mult
 POW = mybir.AluOpType.pow
 ACT = mybir.ActivationFunctionType
 
-CHUNKS = [2, 2, 4, 8, 8, 8]
+CHUNKS = [1, 2, 4, 8, 8, 8, 1]
+
+GROUPS = [1] + [2] * 15 + [1]
+FIRST = [sum(GROUPS[:g]) for g in range(len(GROUPS))]
+ORDER = [('empty_projection', 1), ('turn_back', 1), ('quant_norm', -2), ('copy_attn', 2), ('normalise', 0), ('gain_bias', -1), ('residual', 1), ('project2', -2), ('quant_attn', 2), ('turn_norm', 0), ('interleave', -1), ('deviations', 1), ('gelu', -4), ('widen', 4), ('project', 2), ('bias2', -2), ('turn_attn', 3)]
 
 
 def tile_transformerblock_pb_t_w4_kernel(
@@ -132,52 +134,48 @@ def tile_transformerblock_pb_t_w4_kernel(
         hvs = {}
 
         def widen(g):
-            t = work.tile([P, NT * D], BF16, name="att", align_bytes=64)
+            n = GROUPS[g]
+            t = work.tile([P, n * D], BF16, name="att", align_bytes=64)
             att[g] = t
-            bt, j0 = byte_tiles[NT * g]
-            if g == 0:
-                for j in range(NT):
-                    nc.vector.tensor_tensor(
-                        out=t[:, j * D : (j + 1) * D],
-                        in0=bt[:, (j0 + j) * D : (j0 + j + 1) * D].bitcast(FP8),
-                        in1=scale_t[:, 0, :],
-                        op=MULT,
-                    )
-            else:
-                nc.vector.tensor_tensor(
-                    out=t[:],
-                    in0=bt[:, j0 * D : (j0 + NT) * D].bitcast(FP8),
-                    in1=scale_t[:].rearrange("p j k -> p (j k)"),
-                    op=MULT,
-                )
+            bt, j0 = byte_tiles[FIRST[g]]
+            nc.vector.tensor_tensor(
+                out=t[:],
+                in0=bt[:, j0 * D : (j0 + n) * D].bitcast(FP8),
+                in1=scale_t[:, 0:n, :].rearrange("p j k -> p (j k)"),
+                op=MULT,
+            )
 
         def turn_attn(g):
-            t = psum.tile([P, NT, 2, P], F32, tag="at", name="at")
+            n = GROUPS[g]
+            t = psum.tile([P, n, 2, P], F32, tag="at", name="at")
             atp[g] = t
             words = att[g][:].bitcast(F32)
-            for j in range(NT):
+            for j in range(n):
                 for u in range(2):
                     nc.tensor.transpose(t[:, j, u, :], words[:, 256 * j + u : 256 * (j + 1) : 2], ident[:])
 
         def copy_attn(g):
-            t = work.tile([P, W * PACK], BF16, name="grp", align_bytes=64)
+            n = GROUPS[g]
+            t = work.tile([P, n * P * PACK], BF16, name="grp", align_bytes=64)
             att[g] = t
             nc.scalar.copy(
-                out=t[:].bitcast(F32).rearrange("p (j r u) -> p j r u", j=NT, u=2),
+                out=t[:].bitcast(F32).rearrange("p (j r u) -> p j r u", j=n, u=2),
                 in_=atp[g][:].rearrange("p j u r -> p j r u"),
             )
 
         def quant_attn(g):
-            c = work.tile([P, W], U32, name="c1", align_bytes=64)
-            s = work.tile([P, W], U8, name="s1", align_bytes=64)
+            n = GROUPS[g]
+            c = work.tile([P, n * P], U32, name="c1", align_bytes=64)
+            s = work.tile([P, n * P], U8, name="s1", align_bytes=64)
             codes[g] = (c, s)
             nc.vector.quantize_mx(out=c[:].bitcast(FP8X4), scales=s[:], in_=att[g][:])
 
         def project(g):
+            n = GROUPS[g]
             c, s = codes[g]
             ptp[g] = []
             for h in range(2):
-                t = psum.tile([P, 2, W], F32, tag="pt", bufs=2, name="pt")
+                t = psum.tile([P, 2, n * P], F32, tag="pt", bufs=2, name="pt")
                 ptp[g].append(t)
                 for e in range(2):
                     blk = 2 * h + e
@@ -192,7 +190,8 @@ def tile_transformerblock_pb_t_w4_kernel(
                     )
 
         def empty_projection(g):
-            t = work.tile([P, 4, W], F32, name="pts")
+            n = GROUPS[g]
+            t = work.tile([P, 4, n * P], F32, name="pts")
             pts[g] = t
             for blk in range(4):
                 nc.scalar.activation(
@@ -200,20 +199,22 @@ def tile_transformerblock_pb_t_w4_kernel(
                 )
 
         def turn_back(g):
+            n = GROUPS[g]
             xmp[g] = []
-            for j in range(NT):
+            for j in range(n):
                 t = psum.tile([P, D], F32, tag="xm", bufs=2, name="xm")
                 xmp[g].append(t)
                 for blk in range(4):
                     nc.tensor.transpose(t[:, P * blk : P * (blk + 1)], pts[g][:, blk, P * j : P * (j + 1)], ident[:])
 
         def residual(g):
-            t = work.tile([P, NT, D], F32, name="mid")
-            s = work.tile([P, NT], F32, name="sums")
+            n = GROUPS[g]
+            t = work.tile([P, n, D], F32, name="mid", bufs=4)
+            s = work.tile([P, n], F32, name="sums", bufs=4)
             xms[g] = t
             stat[g] = s
-            for j in range(NT):
-                xt, jj = x_tiles[NT * g + j]
+            for j in range(n):
+                xt, jj = x_tiles[FIRST[g] + j]
                 nc.vector.scalar_tensor_tensor(
                     out=t[:, j, :],
                     in0=xmp[g][j][:],
@@ -223,11 +224,12 @@ def tile_transformerblock_pb_t_w4_kernel(
                     op1=ADD,
                     accum_out=s[:, j : j + 1],
                 )
-            nc.sync.dma_start(out=mid_v[:, NT * g : NT * (g + 1), :], in_=t[:])
+            nc.sync.dma_start(out=mid_v[:, FIRST[g] : FIRST[g] + n, :], in_=t[:])
 
         def deviations(g):
-            sq = work.tile([P, NT], F32, name="sq")
-            for j in range(NT):
+            n = GROUPS[g]
+            sq = work.tile([P, n], F32, name="sq", bufs=4)
+            for j in range(n):
                 junk = work.tile([P, D], BF16, name="junk", bufs=2)
                 nc.scalar.activation(
                     out=junk[:],
@@ -237,19 +239,20 @@ def tile_transformerblock_pb_t_w4_kernel(
                     bias=stat[g][:, j : j + 1],
                     accum_out=sq[:, j : j + 1],
                 )
-            mean = work.tile([P, NT], F32, name="mean")
+            mean = work.tile([P, n], F32, name="mean", bufs=4)
             nc.gpsimd.tensor_scalar(out=mean[:], in0=stat[g][:], scalar1=1.0 / D, scalar2=0.0, op0=MULT, op1=ADD)
-            var = work.tile([P, NT], F32, name="var")
+            var = work.tile([P, n], F32, name="var", bufs=4)
             nc.gpsimd.tensor_scalar(out=var[:], in0=sq[:], scalar1=1.0 / D**3, scalar2=EPS, op0=MULT, op1=ADD)
-            rstd = work.tile([P, NT], F32, name="rstd")
-            nc.gpsimd.tensor_tensor(out=rstd[:], in0=var[:], in1=expo[:], op=POW)
+            rstd = work.tile([P, n], F32, name="rstd", bufs=4)
+            nc.gpsimd.tensor_tensor(out=rstd[:], in0=var[:], in1=expo[:, 0:n], op=POW)
             stat[g] = (mean, rstd)
 
         def normalise(g):
-            t = work.tile([P, NT, D], F32, name="xh")
+            n = GROUPS[g]
+            t = work.tile([P, n, D], F32, name="xh")
             xhs[g] = t
             mean, rstd = stat[g]
-            for j in range(NT):
+            for j in range(n):
                 nc.vector.tensor_scalar(
                     out=t[:, j, :].rearrange("p (t m) -> p m t", t=PACK),
                     in0=xms[g][:, j, :].rearrange("p (m t) -> p m t", t=PACK),
@@ -260,19 +263,21 @@ def tile_transformerblock_pb_t_w4_kernel(
                 )
 
         def turn_norm(g):
+            n = GROUPS[g]
             xhp[g] = []
             for h in range(2):
-                t = psum.tile([P, 2, W], F32, tag="xh", bufs=2, name="xhp")
+                t = psum.tile([P, 2, n * P], F32, tag="xh", bufs=2, name="xhp")
                 xhp[g].append(t)
                 for e in range(2):
                     k = 2 * h + e
-                    for j in range(NT):
+                    for j in range(n):
                         nc.tensor.transpose(
                             t[:, e, P * j : P * (j + 1)], xhs[g][:, j, P * k : P * (k + 1)], ident[:]
                         )
 
         def gain_bias(g):
-            t = work.tile([P, PACK, W], BF16, name="planes")
+            n = GROUPS[g]
+            t = work.tile([P, PACK, n * P], BF16, name="planes")
             pls[g] = t
             for k in range(PACK):
                 nc.scalar.activation(
@@ -284,7 +289,8 @@ def tile_transformerblock_pb_t_w4_kernel(
                 )
 
         def interleave(g):
-            t = work.tile([P, W * PACK], BF16, name="hq", align_bytes=64)
+            n = GROUPS[g]
+            t = work.tile([P, n * P * PACK], BF16, name="hq", align_bytes=64)
             hqs[g] = t
             nc.vector.tensor_copy(
                 out=t[:].rearrange("p (c i t) -> p c t i", i=4, t=PACK),
@@ -292,16 +298,29 @@ def tile_transformerblock_pb_t_w4_kernel(
             )
 
         def quant_norm(g):
-            c = work.tile([P, W], U32, name="c2", align_bytes=64)
-            s = work.tile([P, W], U8, name="s2", align_bytes=64)
+            n = GROUPS[g]
+            c = work.tile([P, n * P], U32, name="c2", align_bytes=64)
+            s = work.tile([P, n * P], U8, name="s2", align_bytes=64)
             codes2[g] = (c, s)
             nc.vector.quantize_mx(out=c[:].bitcast(FP8X4), scales=s[:], in_=hqs[g][:])
 
         def project2(g):
+            n = GROUPS[g]
             c, s = codes2[g]
-            t = psum.tile([P, NT, F], F32, tag="hid", name="hp")
+            bank = psum.tile([P, 4, F], F32, tag="hid", name="hp")
+            t = bank[:, 0:n, :]
             hps[g] = t
-            for j in range(NT):
+            for blk in range(4):
+                nc.tensor.matmul_mx(
+                    out=bank[:, 2 : 2 + n, :].rearrange("p j f -> p (j f)"),
+                    lhsT=w_words[:, 256 * blk : 256 * (blk + 1)].bitcast(FP4X4),
+                    lhsT_scale=wscale[:, P * blk : P * (blk + 1)],
+                    rhs=c[:].bitcast(FP8X4),
+                    rhs_scale=s[:],
+                    start=True,
+                    stop=True,
+                )
+            for j in range(n):
                 nc.tensor.matmul_mx(
                     out=t[:, j, :],
                     lhsT=c[:, P * j : P * (j + 1)].bitcast(FP8X4),
@@ -313,35 +332,43 @@ def tile_transformerblock_pb_t_w4_kernel(
                 )
 
         def bias2(g):
-            t = work.tile([P, NT, F], F32, name="hv")
+            n = GROUPS[g]
+            t = work.tile([P, n, F], F32, name="hv")
             hvs[g] = t
-            nc.vector.tensor_tensor(out=t[:], in0=hps[g][:], in1=b1_t[:], op=ADD)
+            nc.vector.tensor_tensor(out=t[:], in0=hps[g], in1=b1_t[:, 0:n, :], op=ADD)
 
         def gelu(g):
-            t = work.tile([P, NT, F], F32, name="ho")
+            n = GROUPS[g]
+            t = work.tile([P, n, F], F32, name="ho")
             nc.scalar.activation(out=t[:], in_=hvs[g][:], func=ACT.Gelu)
-            nc.sync.dma_start(out=hid_v[:, NT * g : NT * (g + 1), :], in_=t[:])
+            nc.sync.dma_start(out=hid_v[:, FIRST[g] : FIRST[g] + n, :], in_=t[:])
 
         def run(step, g):
-            if 0 <= g < GROUPS:
+            if 0 <= g < len(GROUPS):
                 step(g)
 
-        if True:
-            for i in range(-2, GROUPS + 2):
-                run(residual, i)
-                run(gain_bias, i - 1)
-                run(project2, i - 2)
-                run(project, i + 1)
-                run(deviations, i)
-                run(widen, i + 2)
-                run(bias2, i - 2)
-                run(empty_projection, i + 1)
-                run(turn_attn, i + 2)
-                run(interleave, i - 1)
-                run(turn_back, i + 1)
-                run(copy_attn, i + 2)
-                run(normalise, i)
-                run(quant_norm, i - 1)
-                run(gelu, i - 2)
-                run(turn_norm, i)
-                run(quant_attn, i + 2)
+        steps = {
+            "widen": widen,
+            "turn_attn": turn_attn,
+            "copy_attn": copy_attn,
+            "quant_attn": quant_attn,
+            "project": project,
+            "empty_projection": empty_projection,
+            "turn_back": turn_back,
+            "residual": residual,
+            "deviations": deviations,
+            "normalise": normalise,
+            "turn_norm": turn_norm,
+            "gain_bias": gain_bias,
+            "interleave": interleave,
+            "quant_norm": quant_norm,
+            "project2": project2,
+            "bias2": bias2,
+            "gelu": gelu,
+        }
+        ahead = max(o for s, o in ORDER)
+        behind = -min(o for s, o in ORDER)
+        with tc.manual_schedule():
+            for i in range(-ahead, len(GROUPS) + behind):
+                for name, offset in ORDER:
+                    run(steps[name], i + offset)

@@ -60,6 +60,8 @@ def tile_transformerblock_pb_t_w4_kernel(
         make_identity(nc, ident[:])
         expo = keep.tile([P, NT], F32, name="expo")
         nc.gpsimd.memset(expo[:], -0.5)
+        eps_t = keep.tile([P, 1], F32, name="eps_t")
+        nc.vector.memset(eps_t[:], EPS)
         warm = keep.tile([P, 1], F32, name="warm")
         nc.vector.memset(warm[:], 0.0)
         warm_o = keep.tile([P, 1], F32, name="warm_o")
@@ -240,9 +242,9 @@ def tile_transformerblock_pb_t_w4_kernel(
                     accum_out=sq[:, j : j + 1],
                 )
             mean = work.tile([P, n], F32, name="mean", bufs=4)
-            nc.gpsimd.tensor_scalar(out=mean[:], in0=stat[g][:], scalar1=1.0 / D, scalar2=0.0, op0=MULT, op1=ADD)
+            nc.scalar.activation(out=mean[:], in_=stat[g][:], func=ACT.Copy, scale=1.0 / D)
             var = work.tile([P, n], F32, name="var", bufs=4)
-            nc.gpsimd.tensor_scalar(out=var[:], in0=sq[:], scalar1=1.0 / D**3, scalar2=EPS, op0=MULT, op1=ADD)
+            nc.scalar.activation(out=var[:], in_=sq[:], func=ACT.Identity, scale=1.0 / D**3, bias=eps_t[:])
             rstd = work.tile([P, n], F32, name="rstd", bufs=4)
             nc.gpsimd.tensor_tensor(out=rstd[:], in0=var[:], in1=expo[:, 0:n], op=POW)
             stat[g] = (mean, rstd)
@@ -254,8 +256,8 @@ def tile_transformerblock_pb_t_w4_kernel(
             mean, rstd = stat[g]
             for j in range(n):
                 nc.vector.tensor_scalar(
-                    out=t[:, j, :].rearrange("p (t m) -> p m t", t=PACK),
-                    in0=xms[g][:, j, :].rearrange("p (m t) -> p m t", t=PACK),
+                    out=t[:, j, :].rearrange("p (u m e) -> p m u e", u=2, e=2),
+                    in0=xms[g][:, j, :].rearrange("p (m u e) -> p m u e", u=2, e=2),
                     scalar1=mean[:, j : j + 1],
                     scalar2=rstd[:, j : j + 1],
                     op0=SUB,
@@ -269,10 +271,9 @@ def tile_transformerblock_pb_t_w4_kernel(
                 t = psum.tile([P, 2, n * P], F32, tag="xh", bufs=2, name="xhp")
                 xhp[g].append(t)
                 for e in range(2):
-                    k = 2 * h + e
                     for j in range(n):
                         nc.tensor.transpose(
-                            t[:, e, P * j : P * (j + 1)], xhs[g][:, j, P * k : P * (k + 1)], ident[:]
+                            t[:, e, P * j : P * (j + 1)], xhs[g][:, j, 2 * P * h + e : 2 * P * (h + 1) : 2], ident[:]
                         )
 
         def gain_bias(g):
@@ -293,8 +294,8 @@ def tile_transformerblock_pb_t_w4_kernel(
             t = work.tile([P, n * P * PACK], BF16, name="hq", align_bytes=64)
             hqs[g] = t
             nc.vector.tensor_copy(
-                out=t[:].rearrange("p (c i t) -> p c t i", i=4, t=PACK),
-                in_=pls[g][:].rearrange("p t (c i) -> p c t i", i=4),
+                out=t[:].rearrange("p (c t) -> p c t", t=PACK),
+                in_=pls[g][:].rearrange("p t c -> p c t"),
             )
 
         def quant_norm(g):
@@ -310,7 +311,7 @@ def tile_transformerblock_pb_t_w4_kernel(
             bank = psum.tile([P, 4, F], F32, tag="hid", name="hp")
             t = bank[:, 0:n, :]
             hps[g] = t
-            for blk in range(4):
+            for blk in range(2):
                 nc.tensor.matmul_mx(
                     out=bank[:, 2 : 2 + n, :].rearrange("p j f -> p (j f)"),
                     lhsT=w_words[:, 256 * blk : 256 * (blk + 1)].bitcast(FP4X4),

@@ -32,7 +32,8 @@ CHUNKS = [1, 2, 4, 8, 8, 8, 1]
 
 GROUPS = [1] + [2] * 15 + [1]
 FIRST = [sum(GROUPS[:g]) for g in range(len(GROUPS))]
-ORDER = [('empty_projection', 1), ('turn_back', 1), ('quant_norm', -2), ('copy_attn', 2), ('normalise', 0), ('gain_bias', -1), ('residual', 1), ('project2', -2), ('quant_attn', 2), ('turn_norm', 0), ('interleave', -1), ('deviations', 1), ('gelu', -4), ('widen', 4), ('project', 2), ('bias2', -2), ('turn_attn', 3)]
+LATE = 2
+ORDER = [('bias2', -9), ('deviations', -2), ('project2', -8), ('moments', -3), ('interleave', -7), ('residual', -1), ('turn_attn', 3), ('quant_attn', 2), ('gelu', -12), ('gain_bias', -6), ('empty_projection', 1), ('turn_back', 0), ('turn_norm', -5), ('normalise', -4), ('quant_norm', -7), ('widen', 4), ('project', 2), ('copy_attn', 3)]
 
 
 def tile_transformerblock_pb_t_w4_kernel(
@@ -46,11 +47,12 @@ def tile_transformerblock_pb_t_w4_kernel(
 
     with ExitStack() as ctx:
         keep = ctx.enter_context(tc.tile_pool(name="keep", bufs=1))
-        work = ctx.enter_context(tc.tile_pool(name="work", bufs=3))
+        work = ctx.enter_context(tc.tile_pool(name="work", bufs=4))
         psum = ctx.enter_context(tc.psum_pool(name="psum", bufs=1))
 
         scale_t = keep.tile([P, NT, D], F32, name="scale_t", align_bytes=64)
-        nc.scalar.dma_start(out=scale_t[:, 0, :], in_=attn_scale.rearrange("o t k -> (o t k)").partition_broadcast(P))
+        sc4 = keep.tile([P, PACK], F32, name="sc4")
+        nc.scalar.dma_start(out=sc4[:], in_=attn_scale.rearrange("o t (p k) -> p (o t k)", k=PACK))
 
         wscale = keep.tile([P, D + F], U8, name="wscale", align_bytes=64)
         nc.vector.memset(wscale[:].bitcast(I32), 0)
@@ -60,8 +62,6 @@ def tile_transformerblock_pb_t_w4_kernel(
         make_identity(nc, ident[:])
         expo = keep.tile([P, NT], F32, name="expo")
         nc.gpsimd.memset(expo[:], -0.5)
-        eps_t = keep.tile([P, 1], F32, name="eps_t")
-        nc.vector.memset(eps_t[:], EPS)
         warm = keep.tile([P, 1], F32, name="warm")
         nc.vector.memset(warm[:], 0.0)
         warm_o = keep.tile([P, 1], F32, name="warm_o")
@@ -94,6 +94,8 @@ def tile_transformerblock_pb_t_w4_kernel(
             x_t = keep.tile([P, n, D], BF16, name="x%d" % ci)
             nc.sync.dma_start(out=x_t[:], in_=x_v[:, start : start + n, :])
             if ci == 1:
+                nc.sync.dma_start(out=scale_t[:, 0, :], in_=attn_scale.rearrange("o t k -> (o t k)").partition_broadcast(P))
+            if ci == 2:
                 nc.sync.dma_start(out=w1_t[:], in_=w1_words[0])
                 for q in range(4):
                     nc.sync.dma_start(
@@ -127,6 +129,7 @@ def tile_transformerblock_pb_t_w4_kernel(
         xmp = {}
         xms = {}
         stat = {}
+        sqs = {}
         xhs = {}
         xhp = {}
         pls = {}
@@ -140,6 +143,9 @@ def tile_transformerblock_pb_t_w4_kernel(
             t = work.tile([P, n * D], BF16, name="att", align_bytes=64)
             att[g] = t
             bt, j0 = byte_tiles[FIRST[g]]
+            if g < LATE:
+                nc.vector.tensor_copy(out=t[:], in_=bt[:, j0 * D : (j0 + n) * D].bitcast(FP8))
+                return
             nc.vector.tensor_tensor(
                 out=t[:],
                 in0=bt[:, j0 * D : (j0 + n) * D].bitcast(FP8),
@@ -160,6 +166,15 @@ def tile_transformerblock_pb_t_w4_kernel(
             n = GROUPS[g]
             t = work.tile([P, n * P * PACK], BF16, name="grp", align_bytes=64)
             att[g] = t
+            if g < LATE:
+                for j in range(n):
+                    nc.vector.tensor_tensor(
+                        out=t[:, j * D : (j + 1) * D].rearrange("p (r u e) -> p r u e", u=2, e=2),
+                        in0=atp[g][:, j, :, :].bitcast(BF16).rearrange("p u (r e) -> p r u e", e=2),
+                        in1=sc4[:].rearrange("p (o u e) -> p o u e", o=1, u=2).to_broadcast([P, P, 2, 2]),
+                        op=MULT,
+                    )
+                return
             nc.scalar.copy(
                 out=t[:].bitcast(F32).rearrange("p (j r u) -> p j r u", j=n, u=2),
                 in_=atp[g][:].rearrange("p j u r -> p j r u"),
@@ -211,8 +226,8 @@ def tile_transformerblock_pb_t_w4_kernel(
 
         def residual(g):
             n = GROUPS[g]
-            t = work.tile([P, n, D], F32, name="mid", bufs=4)
-            s = work.tile([P, n], F32, name="sums", bufs=4)
+            t = work.tile([P, n, D], F32, name="mid", bufs=6)
+            s = work.tile([P, n], F32, name="sums", bufs=6)
             xms[g] = t
             stat[g] = s
             for j in range(n):
@@ -230,7 +245,7 @@ def tile_transformerblock_pb_t_w4_kernel(
 
         def deviations(g):
             n = GROUPS[g]
-            sq = work.tile([P, n], F32, name="sq", bufs=4)
+            sq = work.tile([P, n], F32, name="sq", bufs=6)
             for j in range(n):
                 junk = work.tile([P, D], BF16, name="junk", bufs=2)
                 nc.scalar.activation(
@@ -241,11 +256,16 @@ def tile_transformerblock_pb_t_w4_kernel(
                     bias=stat[g][:, j : j + 1],
                     accum_out=sq[:, j : j + 1],
                 )
-            mean = work.tile([P, n], F32, name="mean", bufs=4)
-            nc.scalar.activation(out=mean[:], in_=stat[g][:], func=ACT.Copy, scale=1.0 / D)
-            var = work.tile([P, n], F32, name="var", bufs=4)
-            nc.scalar.activation(out=var[:], in_=sq[:], func=ACT.Identity, scale=1.0 / D**3, bias=eps_t[:])
-            rstd = work.tile([P, n], F32, name="rstd", bufs=4)
+            sqs[g] = sq
+
+        def moments(g):
+            n = GROUPS[g]
+            sq = sqs[g]
+            mean = work.tile([P, n], F32, name="mean", bufs=6)
+            nc.vector.tensor_scalar(out=mean[:], in0=stat[g][:], scalar1=1.0 / D, scalar2=None, op0=MULT)
+            var = work.tile([P, n], F32, name="var", bufs=6)
+            nc.vector.tensor_scalar(out=var[:], in0=sq[:], scalar1=1.0 / D**3, scalar2=EPS, op0=MULT, op1=ADD)
+            rstd = work.tile([P, n], F32, name="rstd", bufs=6)
             nc.gpsimd.tensor_tensor(out=rstd[:], in0=var[:], in1=expo[:, 0:n], op=POW)
             stat[g] = (mean, rstd)
 
@@ -358,6 +378,7 @@ def tile_transformerblock_pb_t_w4_kernel(
             "turn_back": turn_back,
             "residual": residual,
             "deviations": deviations,
+            "moments": moments,
             "normalise": normalise,
             "turn_norm": turn_norm,
             "gain_bias": gain_bias,

@@ -62,19 +62,19 @@ def tile_transformerblock_pb_t_w4_kernel(
         make_identity(nc, ident[:])
         expo = keep.tile([P, NT], F32, name="expo")
         nc.gpsimd.memset(expo[:], -0.5)
-        warm = keep.tile([P, 1], F32, name="warm")
-        nc.vector.memset(warm[:], 0.0)
-        warm_o = keep.tile([P, 1], F32, name="warm_o")
-        nc.scalar.activation(out=warm_o[:], in_=warm[:], func=ACT.Gelu)
-
         b_raw = keep.tile([P, P], BF16, name="b_raw")
         nc.scalar.dma_start(out=b_raw[0:4, :], in_=b_out.rearrange("(j m) -> j m", m=P))
+        nc.scalar.dma_start(out=b_raw[4:5, :], in_=b1.rearrange("(j m) -> j m", m=P))
         g_raw = keep.tile([P, PACK], BF16, name="g_raw")
         nc.scalar.dma_start(out=g_raw[:], in_=ln2_g.rearrange("(p t) -> p t", t=PACK))
         lb_raw = keep.tile([P, PACK], BF16, name="lb_raw")
         nc.scalar.dma_start(out=lb_raw[:], in_=ln2_b.rearrange("(p t) -> p t", t=PACK))
-        b1_t = keep.tile([P, NT, F], BF16, name="b1_t")
-        nc.scalar.dma_start(out=b1_t[:, 0, :], in_=b1.partition_broadcast(P))
+        b1_t = keep.tile([P, NT, F], F32, name="b1_t")
+
+        warm = keep.tile([P, 1], F32, name="warm")
+        nc.vector.memset(warm[:], 0.0)
+        warm_o = keep.tile([P, 1], F32, name="warm_o")
+        nc.scalar.activation(out=warm_o[:], in_=warm[:], func=ACT.Gelu)
 
         byte_tiles = []
         x_tiles = []
@@ -93,8 +93,6 @@ def tile_transformerblock_pb_t_w4_kernel(
                     )
             x_t = keep.tile([P, n, D], BF16, name="x%d" % ci)
             nc.sync.dma_start(out=x_t[:], in_=x_v[:, start : start + n, :])
-            if ci == 1:
-                nc.sync.dma_start(out=scale_t[:, 0, :], in_=attn_scale.rearrange("o t k -> (o t k)").partition_broadcast(P))
             if ci == 2:
                 nc.sync.dma_start(out=w1_t[:], in_=w1_words[0])
                 for q in range(4):
@@ -107,19 +105,30 @@ def tile_transformerblock_pb_t_w4_kernel(
                 x_tiles.append((x_t, j))
             start += n
 
-        nc.gpsimd.tensor_copy(out=b_rows[0:4, :], in_=b_raw[0:4, :])
+        nc.gpsimd.tensor_copy(out=b_rows[0:5, :], in_=b_raw[0:5, :])
         g_f = keep.tile([P, PACK], F32, name="g_f")
         nc.gpsimd.tensor_copy(out=g_f[:], in_=g_raw[:])
         lb_f = keep.tile([P, PACK], F32, name="lb_f")
         nc.gpsimd.tensor_copy(out=lb_f[:], in_=lb_raw[:])
-        for j in range(1, NT):
-            nc.gpsimd.tensor_copy(out=b1_t[:, j, :], in_=b1_t[:, 0, :])
-        bp = psum.tile([P, P], F32, tag="hid", name="bp")
-        nc.tensor.transpose(bp[:], b_rows[:], ident[:])
-        b_col = keep.tile([P, PACK], F32, name="b_col")
-        nc.scalar.copy(out=b_col[:], in_=bp[:, 0:PACK])
-        for j in range(1, NT):
-            nc.scalar.copy(out=scale_t[:, j, :], in_=scale_t[:, 0, :])
+        b_col = keep.tile([P, PACK + 1], F32, name="b_col")
+
+        def spread_scales():
+            t = psum.tile([P, PACK, P], F32, tag="hid", name="sp")
+            for k in range(PACK):
+                nc.tensor.transpose(t[:, k, :], sc4[:, k : k + 1].to_broadcast([P, P]), ident[:])
+            for j in range(NT):
+                nc.scalar.copy(out=scale_t[:, j, :].rearrange("p (m t) -> p m t", t=PACK), in_=t[:].rearrange("p t m -> p m t"))
+
+        def spread_biases():
+            bp = psum.tile([P, P], F32, tag="hid", name="bp")
+            nc.tensor.transpose(bp[:], b_rows[:], ident[:])
+            nc.scalar.copy(out=b_col[:], in_=bp[:, 0 : PACK + 1])
+
+        def spread_b1():
+            t = psum.tile([P, P], F32, tag="hid", name="b1p")
+            nc.tensor.transpose(t[:], b_col[:, PACK : PACK + 1].to_broadcast([P, P]), ident[:])
+            for j in range(NT):
+                nc.scalar.copy(out=b1_t[:, j, :], in_=t[:])
 
         att = {}
         atp = {}
@@ -194,8 +203,7 @@ def tile_transformerblock_pb_t_w4_kernel(
             for h in range(2):
                 t = psum.tile([P, 2, n * P], F32, tag="pt", bufs=2, name="pt")
                 ptp[g].append(t)
-                for e in range(2):
-                    blk = 2 * h + e
+                for e, blk in ((0, 2 * h), (0, 2 * h), (1, 2 * h + 1)):
                     nc.tensor.matmul_mx(
                         out=t[:, e, :],
                         lhsT=w_words[:, 256 * blk : 256 * (blk + 1)].bitcast(FP4X4),
@@ -314,8 +322,8 @@ def tile_transformerblock_pb_t_w4_kernel(
             t = work.tile([P, n * P * PACK], BF16, name="hq", align_bytes=64)
             hqs[g] = t
             nc.vector.tensor_copy(
-                out=t[:].rearrange("p (c t) -> p c t", t=PACK),
-                in_=pls[g][:].rearrange("p t c -> p c t"),
+                out=t[:].rearrange("p (c i t) -> p c t i", i=4, t=PACK),
+                in_=pls[g][:].rearrange("p t (c i) -> p c t i", i=4),
             )
 
         def quant_norm(g):
@@ -328,19 +336,8 @@ def tile_transformerblock_pb_t_w4_kernel(
         def project2(g):
             n = GROUPS[g]
             c, s = codes2[g]
-            bank = psum.tile([P, 4, F], F32, tag="hid", name="hp")
-            t = bank[:, 0:n, :]
+            t = psum.tile([P, n, F], F32, tag="hid", name="hp")
             hps[g] = t
-            for blk in range(2):
-                nc.tensor.matmul_mx(
-                    out=bank[:, 2 : 2 + n, :].rearrange("p j f -> p (j f)"),
-                    lhsT=w_words[:, 256 * blk : 256 * (blk + 1)].bitcast(FP4X4),
-                    lhsT_scale=wscale[:, P * blk : P * (blk + 1)],
-                    rhs=c[:].bitcast(FP8X4),
-                    rhs_scale=s[:],
-                    start=True,
-                    stop=True,
-                )
             for j in range(n):
                 nc.tensor.matmul_mx(
                     out=t[:, j, :],
@@ -356,7 +353,7 @@ def tile_transformerblock_pb_t_w4_kernel(
             n = GROUPS[g]
             t = work.tile([P, n, F], F32, name="hv")
             hvs[g] = t
-            nc.vector.tensor_tensor(out=t[:], in0=hps[g], in1=b1_t[:, 0:n, :], op=ADD)
+            nc.vector.tensor_tensor(out=t[:], in0=hps[g][:], in1=b1_t[:, 0:n, :], op=ADD)
 
         def gelu(g):
             n = GROUPS[g]
@@ -394,3 +391,9 @@ def tile_transformerblock_pb_t_w4_kernel(
             for i in range(-ahead, len(GROUPS) + behind):
                 for name, offset in ORDER:
                     run(steps[name], i + offset)
+                if i == -ahead:
+                    spread_scales()
+                if i == 1 - ahead:
+                    spread_biases()
+                if i == 0:
+                    spread_b1()

from contextlib import ExitStack

import concourse.mybir as mybir
from concourse.masks import make_identity

P = 128
PACK = 4
D = 512
F = 128
TOKENS = 4096
TILES = TOKENS // P
NT = 2
EPS = 1e-5

FLOPS = 2 * TOKENS * D * D + 2 * TOKENS * D * F

F32 = mybir.dt.float32
BF16 = mybir.dt.bfloat16
U32 = mybir.dt.uint32
I32 = mybir.dt.int32
U8 = mybir.dt.uint8
FP8 = mybir.dt.float8_e4m3fn
FP8X4 = mybir.dt.float8_e4m3fn_x4
FP4X4 = mybir.dt.float4_e2m1fn_x4
ADD = mybir.AluOpType.add
SUB = mybir.AluOpType.subtract
MULT = mybir.AluOpType.mult
POW = mybir.AluOpType.pow
ACT = mybir.ActivationFunctionType

CHUNKS = [1, 2, 4, 8, 8, 8, 1]

GROUPS = [1] + [2] * 15 + [1]
FIRST = [sum(GROUPS[:g]) for g in range(len(GROUPS))]
LATE = 2
ORDER = [('bias2', -9), ('deviations', -2), ('project2', -8), ('moments', -3), ('interleave', -7), ('residual', -1), ('turn_attn', 3), ('quant_attn', 2), ('gelu', -12), ('gain_bias', -6), ('empty_projection', 1), ('turn_back', 0), ('turn_norm', -5), ('normalise', -4), ('quant_norm', -7), ('widen', 4), ('project', 2), ('copy_attn', 3)]


def tile_transformerblock_pb_t_w4_kernel(
    tc, attn_bytes, attn_scale, x, w_out_words, w_out_scales, b_out, ln2_g, ln2_b, w1_words, w1_scales, b1, out_0, out_1
):
    nc = tc.nc
    bytes_v = attn_bytes.rearrange("b t k -> (b t) k").rearrange("(p j) k -> p j k", p=P)
    x_v = x.rearrange("b t d -> (b t) d").rearrange("(p j) d -> p j d", p=P)
    mid_v = out_0.rearrange("b t d -> (b t) d").rearrange("(p j) d -> p j d", p=P)
    hid_v = out_1.rearrange("b t f -> (b t) f").rearrange("(p j) f -> p j f", p=P)

    with ExitStack() as ctx:
        keep = ctx.enter_context(tc.tile_pool(name="keep", bufs=1))
        work = ctx.enter_context(tc.tile_pool(name="work", bufs=4))
        psum = ctx.enter_context(tc.psum_pool(name="psum", bufs=1))

        scale_t = keep.tile([P, NT, D], F32, name="scale_t", align_bytes=64)
        sc4 = keep.tile([P, PACK], F32, name="sc4")
        nc.scalar.dma_start(out=sc4[:], in_=attn_scale.rearrange("o t (p k) -> p (o t k)", k=PACK))

        wscale = keep.tile([P, D + F], U8, name="wscale", align_bytes=64)
        nc.vector.memset(wscale[:].bitcast(I32), 0)
        b_rows = keep.tile([P, P], F32, name="b_rows")
        nc.vector.memset(b_rows[:], 0.0)
        ident = keep.tile([P, P], F32, name="ident")
        make_identity(nc, ident[:])
        expo = keep.tile([P, NT], F32, name="expo")
        nc.gpsimd.memset(expo[:], -0.5)
        b_raw = keep.tile([P, P], BF16, name="b_raw")
        nc.scalar.dma_start(out=b_raw[0:4, :], in_=b_out.rearrange("(j m) -> j m", m=P))
        nc.scalar.dma_start(out=b_raw[4:5, :], in_=b1.rearrange("(j m) -> j m", m=P))
        g_raw = keep.tile([P, PACK], BF16, name="g_raw")
        nc.scalar.dma_start(out=g_raw[:], in_=ln2_g.rearrange("(p t) -> p t", t=PACK))
        lb_raw = keep.tile([P, PACK], BF16, name="lb_raw")
        nc.scalar.dma_start(out=lb_raw[:], in_=ln2_b.rearrange("(p t) -> p t", t=PACK))
        b1_t = keep.tile([P, NT, F], F32, name="b1_t")

        warm = keep.tile([P, 1], F32, name="warm")
        nc.vector.memset(warm[:], 0.0)
        warm_o = keep.tile([P, 1], F32, name="warm_o")
        nc.scalar.activation(out=warm_o[:], in_=warm[:], func=ACT.Gelu)

        byte_tiles = []
        x_tiles = []
        w_words = keep.tile([P, 2 * D], U8, name="w_words", align_bytes=64)
        w1_t = keep.tile([P, 2 * F], U8, name="w1_t", align_bytes=64)
        start = 0
        for ci, n in enumerate(CHUNKS):
            byte_t = keep.tile([P, n * D], U8, name="bytes%d" % ci, align_bytes=64)
            nc.sync.dma_start(out=byte_t[:].rearrange("p (j k) -> p j k", k=D), in_=bytes_v[:, start : start + n, :])
            if ci == 0:
                nc.sync.dma_start(out=w_words[:], in_=w_out_words[0])
                for q in range(4):
                    nc.sync.dma_start(
                        out=wscale[32 * q : 32 * q + 4, 0:D].bitcast(I32),
                        in_=w_out_scales[0, 4 * q : 4 * q + 4, :].bitcast(I32),
                    )
            x_t = keep.tile([P, n, D], BF16, name="x%d" % ci)
            nc.sync.dma_start(out=x_t[:], in_=x_v[:, start : start + n, :])
            if ci == 2:
                nc.sync.dma_start(out=w1_t[:], in_=w1_words[0])
                for q in range(4):
                    nc.sync.dma_start(
                        out=wscale[32 * q : 32 * q + 4, D : D + F].bitcast(I32),
                        in_=w1_scales[0, 4 * q : 4 * q + 4, :].bitcast(I32),
                    )
            for j in range(n):
                byte_tiles.append((byte_t, j))
                x_tiles.append((x_t, j))
            start += n

        nc.gpsimd.tensor_copy(out=b_rows[0:5, :], in_=b_raw[0:5, :])
        g_f = keep.tile([P, PACK], F32, name="g_f")
        nc.gpsimd.tensor_copy(out=g_f[:], in_=g_raw[:])
        lb_f = keep.tile([P, PACK], F32, name="lb_f")
        nc.gpsimd.tensor_copy(out=lb_f[:], in_=lb_raw[:])
        b_col = keep.tile([P, PACK + 1], F32, name="b_col")

        def spread_scales():
            t = psum.tile([P, PACK, P], F32, tag="hid", name="sp")
            for k in range(PACK):
                nc.tensor.transpose(t[:, k, :], sc4[:, k : k + 1].to_broadcast([P, P]), ident[:])
            for j in range(NT):
                nc.scalar.copy(out=scale_t[:, j, :].rearrange("p (m t) -> p m t", t=PACK), in_=t[:].rearrange("p t m -> p m t"))

        def spread_biases():
            bp = psum.tile([P, P], F32, tag="hid", name="bp")
            nc.tensor.transpose(bp[:], b_rows[:], ident[:])
            nc.scalar.copy(out=b_col[:], in_=bp[:, 0 : PACK + 1])

        def spread_b1():
            t = psum.tile([P, P], F32, tag="hid", name="b1p")
            nc.tensor.transpose(t[:], b_col[:, PACK : PACK + 1].to_broadcast([P, P]), ident[:])
            for j in range(NT):
                nc.scalar.copy(out=b1_t[:, j, :], in_=t[:])

        att = {}
        atp = {}
        codes = {}
        ptp = {}
        pts = {}
        xmp = {}
        xms = {}
        stat = {}
        sqs = {}
        xhs = {}
        xhp = {}
        pls = {}
        hqs = {}
        codes2 = {}
        hps = {}
        hvs = {}

        def widen(g):
            n = GROUPS[g]
            t = work.tile([P, n * D], BF16, name="att", align_bytes=64)
            att[g] = t
            bt, j0 = byte_tiles[FIRST[g]]
            if g < LATE:
                nc.vector.tensor_copy(out=t[:], in_=bt[:, j0 * D : (j0 + n) * D].bitcast(FP8))
                return
            nc.vector.tensor_tensor(
                out=t[:],
                in0=bt[:, j0 * D : (j0 + n) * D].bitcast(FP8),
                in1=scale_t[:, 0:n, :].rearrange("p j k -> p (j k)"),
                op=MULT,
            )

        def turn_attn(g):
            n = GROUPS[g]
            t = psum.tile([P, n, 2, P], F32, tag="at", name="at")
            atp[g] = t
            words = att[g][:].bitcast(F32)
            for j in range(n):
                for u in range(2):
                    nc.tensor.transpose(t[:, j, u, :], words[:, 256 * j + u : 256 * (j + 1) : 2], ident[:])

        def copy_attn(g):
            n = GROUPS[g]
            t = work.tile([P, n * P * PACK], BF16, name="grp", align_bytes=64)
            att[g] = t
            if g < LATE:
                for j in range(n):
                    nc.vector.tensor_tensor(
                        out=t[:, j * D : (j + 1) * D].rearrange("p (r u e) -> p r u e", u=2, e=2),
                        in0=atp[g][:, j, :, :].bitcast(BF16).rearrange("p u (r e) -> p r u e", e=2),
                        in1=sc4[:].rearrange("p (o u e) -> p o u e", o=1, u=2).to_broadcast([P, P, 2, 2]),
                        op=MULT,
                    )
                return
            nc.scalar.copy(
                out=t[:].bitcast(F32).rearrange("p (j r u) -> p j r u", j=n, u=2),
                in_=atp[g][:].rearrange("p j u r -> p j r u"),
            )

        def quant_attn(g):
            n = GROUPS[g]
            c = work.tile([P, n * P], U32, name="c1", align_bytes=64)
            s = work.tile([P, n * P], U8, name="s1", align_bytes=64)
            codes[g] = (c, s)
            nc.vector.quantize_mx(out=c[:].bitcast(FP8X4), scales=s[:], in_=att[g][:])

        def project(g):
            n = GROUPS[g]
            c, s = codes[g]
            ptp[g] = []
            for h in range(2):
                t = psum.tile([P, 2, n * P], F32, tag="pt", bufs=2, name="pt")
                ptp[g].append(t)
                for e, blk in ((0, 2 * h), (0, 2 * h), (1, 2 * h + 1)):
                    nc.tensor.matmul_mx(
                        out=t[:, e, :],
                        lhsT=w_words[:, 256 * blk : 256 * (blk + 1)].bitcast(FP4X4),
                        lhsT_scale=wscale[:, P * blk : P * (blk + 1)],
                        rhs=c[:].bitcast(FP8X4),
                        rhs_scale=s[:],
                        start=True,
                        stop=True,
                    )

        def empty_projection(g):
            n = GROUPS[g]
            t = work.tile([P, 4, n * P], F32, name="pts")
            pts[g] = t
            for blk in range(4):
                nc.scalar.activation(
                    out=t[:, blk, :], in_=ptp[g][blk // 2][:, blk % 2, :], func=ACT.Identity, bias=b_col[:, blk : blk + 1]
                )

        def turn_back(g):
            n = GROUPS[g]
            xmp[g] = []
            for j in range(n):
                t = psum.tile([P, D], F32, tag="xm", bufs=2, name="xm")
                xmp[g].append(t)
                for blk in range(4):
                    nc.tensor.transpose(t[:, P * blk : P * (blk + 1)], pts[g][:, blk, P * j : P * (j + 1)], ident[:])

        def residual(g):
            n = GROUPS[g]
            t = work.tile([P, n, D], F32, name="mid", bufs=6)
            s = work.tile([P, n], F32, name="sums", bufs=6)
            xms[g] = t
            stat[g] = s
            for j in range(n):
                xt, jj = x_tiles[FIRST[g] + j]
                nc.vector.scalar_tensor_tensor(
                    out=t[:, j, :],
                    in0=xmp[g][j][:],
                    scalar=0.0,
                    in1=xt[:, jj, :],
                    op0=ADD,
                    op1=ADD,
                    accum_out=s[:, j : j + 1],
                )
            nc.sync.dma_start(out=mid_v[:, FIRST[g] : FIRST[g] + n, :], in_=t[:])

        def deviations(g):
            n = GROUPS[g]
            sq = work.tile([P, n], F32, name="sq", bufs=6)
            for j in range(n):
                junk = work.tile([P, D], BF16, name="junk", bufs=2)
                nc.scalar.activation(
                    out=junk[:],
                    in_=xms[g][:, j, :],
                    func=ACT.Square,
                    scale=-float(D),
                    bias=stat[g][:, j : j + 1],
                    accum_out=sq[:, j : j + 1],
                )
            sqs[g] = sq

        def moments(g):
            n = GROUPS[g]
            sq = sqs[g]
            mean = work.tile([P, n], F32, name="mean", bufs=6)
            nc.vector.tensor_scalar(out=mean[:], in0=stat[g][:], scalar1=1.0 / D, scalar2=None, op0=MULT)
            var = work.tile([P, n], F32, name="var", bufs=6)
            nc.vector.tensor_scalar(out=var[:], in0=sq[:], scalar1=1.0 / D**3, scalar2=EPS, op0=MULT, op1=ADD)
            rstd = work.tile([P, n], F32, name="rstd", bufs=6)
            nc.gpsimd.tensor_tensor(out=rstd[:], in0=var[:], in1=expo[:, 0:n], op=POW)
            stat[g] = (mean, rstd)

        def normalise(g):
            n = GROUPS[g]
            t = work.tile([P, n, D], F32, name="xh")
            xhs[g] = t
            mean, rstd = stat[g]
            for j in range(n):
                nc.vector.tensor_scalar(
                    out=t[:, j, :].rearrange("p (u m e) -> p m u e", u=2, e=2),
                    in0=xms[g][:, j, :].rearrange("p (m u e) -> p m u e", u=2, e=2),
                    scalar1=mean[:, j : j + 1],
                    scalar2=rstd[:, j : j + 1],
                    op0=SUB,
                    op1=MULT,
                )

        def turn_norm(g):
            n = GROUPS[g]
            xhp[g] = []
            for h in range(2):
                t = psum.tile([P, 2, n * P], F32, tag="xh", bufs=2, name="xhp")
                xhp[g].append(t)
                for e in range(2):
                    for j in range(n):
                        nc.tensor.transpose(
                            t[:, e, P * j : P * (j + 1)], xhs[g][:, j, 2 * P * h + e : 2 * P * (h + 1) : 2], ident[:]
                        )

        def gain_bias(g):
            n = GROUPS[g]
            t = work.tile([P, PACK, n * P], BF16, name="planes")
            pls[g] = t
            for k in range(PACK):
                nc.scalar.activation(
                    out=t[:, k, :],
                    in_=xhp[g][k // 2][:, k % 2, :],
                    func=ACT.Identity,
                    scale=g_f[:, k : k + 1],
                    bias=lb_f[:, k : k + 1],
                )

        def interleave(g):
            n = GROUPS[g]
            t = work.tile([P, n * P * PACK], BF16, name="hq", align_bytes=64)
            hqs[g] = t
            nc.vector.tensor_copy(
                out=t[:].rearrange("p (c i t) -> p c t i", i=4, t=PACK),
                in_=pls[g][:].rearrange("p t (c i) -> p c t i", i=4),
            )

        def quant_norm(g):
            n = GROUPS[g]
            c = work.tile([P, n * P], U32, name="c2", align_bytes=64)
            s = work.tile([P, n * P], U8, name="s2", align_bytes=64)
            codes2[g] = (c, s)
            nc.vector.quantize_mx(out=c[:].bitcast(FP8X4), scales=s[:], in_=hqs[g][:])

        def project2(g):
            n = GROUPS[g]
            c, s = codes2[g]
            t = psum.tile([P, n, F], F32, tag="hid", name="hp")
            hps[g] = t
            for j in range(n):
                nc.tensor.matmul_mx(
                    out=t[:, j, :],
                    lhsT=c[:, P * j : P * (j + 1)].bitcast(FP8X4),
                    lhsT_scale=s[:, P * j : P * (j + 1)],
                    rhs=w1_t[:].bitcast(FP4X4),
                    rhs_scale=wscale[:, D : D + F],
                    start=True,
                    stop=True,
                )

        def bias2(g):
            n = GROUPS[g]
            t = work.tile([P, n, F], F32, name="hv")
            hvs[g] = t
            nc.vector.tensor_tensor(out=t[:], in0=hps[g][:], in1=b1_t[:, 0:n, :], op=ADD)

        def gelu(g):
            n = GROUPS[g]
            t = work.tile([P, n, F], F32, name="ho")
            nc.scalar.activation(out=t[:], in_=hvs[g][:], func=ACT.Gelu)
            nc.sync.dma_start(out=hid_v[:, FIRST[g] : FIRST[g] + n, :], in_=t[:])

        def run(step, g):
            if 0 <= g < len(GROUPS):
                step(g)

        steps = {
            "widen": widen,
            "turn_attn": turn_attn,
            "copy_attn": copy_attn,
            "quant_attn": quant_attn,
            "project": project,
            "empty_projection": empty_projection,
            "turn_back": turn_back,
            "residual": residual,
            "deviations": deviations,
            "moments": moments,
            "normalise": normalise,
            "turn_norm": turn_norm,
            "gain_bias": gain_bias,
            "interleave": interleave,
            "quant_norm": quant_norm,
            "project2": project2,
            "bias2": bias2,
            "gelu": gelu,
        }
        ahead = max(o for s, o in ORDER)
        behind = -min(o for s, o in ORDER)
        with tc.manual_schedule():
            for i in range(-ahead, len(GROUPS) + behind):
                for name, offset in ORDER:
                    run(steps[name], i + offset)
                if i == -ahead:
                    spread_scales()
                if i == 1 - ahead:
                    spread_biases()
                if i == 0:
                    spread_b1()
